import numpy as np
import ml_dtypes


BF16 = ml_dtypes.bfloat16


def bf(x):
    return np.asarray(x, np.float32).astype(BF16)


def f64(x):
    return np.asarray(x).astype(np.float64)


E2M1 = np.array([0.0, 0.5, 1.0, 1.5, 2.0, 3.0, 4.0, 6.0, -0.0, -0.5, -1.0, -1.5, -2.0, -3.0, -4.0, -6.0])


def pack_weight(w, fmt):
    k, n = w.shape
    w = f64(bf(w)).reshape(k // 32, 32, n)
    amax = np.abs(w).max(1)
    if fmt == "e4m3":
        byte = np.frexp(amax)[1] - 1 + 127 - 7
    else:
        mant, ex = np.frexp(amax / 6.0)
        byte = np.where(mant > 0.5, ex, ex - 1) + 127
    byte = np.clip(np.where(amax > 0, byte, 1), 1, 254)
    scaled = (w * np.exp2(127.0 - byte)[:, None, :]).reshape(k, n).astype(np.float32)
    by_word = np.ascontiguousarray(scaled.reshape(k // 512, 128, 4, n).transpose(0, 1, 3, 2))
    if fmt == "e4m3":
        words = by_word.astype(ml_dtypes.float8_e4m3fn).view(np.uint8)
    else:
        c = by_word.astype(ml_dtypes.float4_e2m1fn).view(np.uint8) & 0xF
        words = c[..., 0::2] | (c[..., 1::2] << 4)
    return np.ascontiguousarray(words), np.ascontiguousarray(byte.astype(np.uint8).reshape(k // 512, 16, n))


def unpack_weight(words, scales, fmt):
    g, p, n, _ = words.shape
    if fmt == "e4m3":
        vals = np.ascontiguousarray(words).view(ml_dtypes.float8_e4m3fn).astype(np.float64)
    else:
        nib = np.empty((g, p, n, 4), np.uint8)
        nib[..., 0::2] = words & 0xF
        nib[..., 1::2] = words >> 4
        vals = E2M1[nib]
    vals = vals * np.repeat(np.exp2(scales.astype(np.float64) - 127.0), 8, axis=1)[..., None]
    return vals.transpose(0, 1, 3, 2).reshape(g * 512, n)

def pack4(w):
    words, scales = pack_weight(w, "e2m1")
    return words.reshape(words.shape[0], 128, -1), scales


def unpack4(words, scales):
    return unpack_weight(words.reshape(words.shape[0], 128, -1, 2), scales, "e2m1")


def kspread(k):
    return np.exp2(np.repeat(np.random.randint(-6, 7, k // 32), 32).astype(np.float64))


B, H, L, E, QD = 32, 1, 128, 4096, 128
EPS = 1e-5


def build_decay_mask(num_heads, max_len):
    r = f64(np.arange(max_len))
    dec = np.array([1.0 - 2.0 ** (-5 - h) for h in range(num_heads)])
    expo = r[None, :] - r[:, None]
    return np.where(r[:, None] >= r[None, :], dec[:, None, None] ** expo[None], 0.0)


def setup_inputs():
    s = kspread(E)
    kv = (0.1 + 0.32 * np.random.standard_normal((B, H, L, QD))) * (0.1 + 0.32 * np.random.standard_normal((B, H, L, QD)))
    x = np.random.standard_normal((B, H, L, E)) * s
    x_words, x_scales = pack4(np.ascontiguousarray(x.reshape(B * H * L, E).T))
    Wq = np.random.standard_normal((QD, E)) / np.sqrt(E) / s
    Wq_words, Wq_scales = pack4(np.ascontiguousarray(Wq.T))
    return {"x_words": x_words,
            "x_scales": x_scales,
            "Wq_words": Wq_words,
            "Wq_scales": Wq_scales,
            "bq": bf(0.3 + 0.3 * np.random.standard_normal(QD)),
            "kv": bf(kv),
            "decay_mask": bf(build_decay_mask(H, L))}


def reference(x_words, x_scales, Wq_words, Wq_scales, bq, kv, decay_mask):
    b, h, l, e = B, H, L, E
    xq = unpack4(x_words, x_scales).T.reshape(b, h, l, e)
    Q = (xq @ unpack4(Wq_words, Wq_scales)) + f64(bq)
    D = f64(decay_mask)[0, :l, :l]
    y = Q * (f64(kv) @ D.T)
    mean = y.mean(axis=(2, 3), keepdims=True)
    var = ((y - mean) ** 2).mean(axis=(2, 3), keepdims=True)
    y = (y - mean) / np.sqrt(var + EPS)
    return y.reshape(b, l, -1)

@@ -1,0 +1,301 @@
+from contextlib import ExitStack
+
+import concourse.mybir as mybir
+from concourse.masks import make_block_diagonal, make_identity
+
+F32 = mybir.dt.float32
+BF16 = mybir.dt.bfloat16
+U8 = mybir.dt.uint8
+I32 = mybir.dt.int32
+FP4X4 = mybir.dt.float4_e2m1fn_x4
+ALU = mybir.AluOpType
+ACT = mybir.ActivationFunctionType
+AX = mybir.AxisListType
+
+P = 128
+PASSES = 8
+ROWS = 4096
+CH = 512
+NCH = ROWS // CH
+T = CH // P
+Q = P // T
+PLANE = 2048
+EPS = 1e-5
+TURN_AFTER = 8
+NORM_AFTER = 10
+FLOPS = 2 * 4096 * 4096 * 128 + 2 * 4096 * 128 * 128
+
+GROUPS = (
+    ((0, 1), ((0, 2), (2, 4), (4, 6), (6, 8))),
+    ((2, 3), ((0, 2), (2, 4), (4, 6), (6, 8))),
+    ((4, 5), ((0, 2), (2, 4), (4, 6), (6, 8))),
+    ((6,), ((0, 2), (2, 4), (4, 6), (6, 8))),
+    ((7,), ((0, 2), (2, 4), (4, 6), (6, 7), (7, 8))),
+)
+
+
+def tile_parallelretention_pb_kernel(
+    tc, x_words, x_scales, Wq_words, Wq_scales, bq, kv, decay_mask, out
+):
+    nc = tc.nc
+    kv_v = kv.rearrange("b h l i -> (b h l) i").rearrange("(c p t) i -> p c (t i)", p=P, t=T)
+    out_v = out.rearrange("b l j -> (b l) j").rearrange("(c p t) j -> p c (t j)", p=P, t=T)
+
+    with ExitStack() as ctx:
+        const = ctx.enter_context(tc.tile_pool(name="const", bufs=1))
+        work = ctx.enter_context(tc.tile_pool(name="work", bufs=3))
+        psum = ctx.enter_context(tc.psum_pool(name="psum", bufs=1))
+
+        ident_bf = const.tile([P, P], BF16, name="ident_bf")
+        ident_f = const.tile([P, P], F32, name="ident_f")
+        blk = const.tile([P, P], F32, name="blk")
+        make_identity(nc, ident_bf[:])
+        make_identity(nc, ident_f[:])
+        make_block_diagonal(nc, blk[:], Q)
+
+        one = const.tile([P, 1], F32, name="one")
+        junk = const.tile([P, 1], F32, name="junk")
+        eps_t = const.tile([P, 1], F32, name="eps_t")
+        ones = const.tile([P, P], F32, name="ones")
+        sel = const.tile([P, T, 2], F32, name="sel")
+        d_sb = const.tile([P, P], BF16, name="d_sb")
+        dT_sb = const.tile([P, P], BF16, name="dT_sb")
+        bq_sb = const.tile([P, 1], BF16, name="bq_sb")
+        kv_sb = const.tile([P, NCH, CH], BF16, name="kv_sb")
+        w_codes = const.tile([P, PASSES, 2 * P], U8, name="w_codes", align_bytes=64)
+        w_plane = const.tile([P, PASSES, P], U8, name="w_plane", align_bytes=64)
+        x_codes = []
+        for u, (chunks, loads) in enumerate(GROUPS):
+            cols = CH * len(chunks)
+            xc = const.tile([P, PASSES, 2 * cols], U8, name="x_codes%d" % u, align_bytes=64)
+            x_codes.append(xc)
+        x_plane = []
+        for v in range(ROWS // PLANE):
+            xp = const.tile([P, PASSES, PLANE], U8, name="x_plane%d" % v, align_bytes=64)
+            x_plane.append(xp)
+        kvT_sb = []
+        gT_sb = []
+        o_sb = []
+        for c in range(NCH):
+            kt = const.tile([P, CH], BF16, name="kvT_sb%d" % c)
+            gt = const.tile([P, CH], F32, name="gT_sb%d" % c)
+            ot = const.tile([P, CH], F32, name="o_sb%d" % c)
+            kvT_sb.append(kt)
+            gT_sb.append(gt)
+            o_sb.append(ot)
+
+        ctx.enter_context(tc.manual_schedule())
+
+        nc.scalar.dma_start(out=d_sb[:], in_=decay_mask[0])
+        with nc.allow_non_contiguous_dma(reason="one bias value to a partition"):
+            nc.scalar.dma_start(out=bq_sb[:], in_=bq.rearrange("(p o) -> p o", o=1))
+        nc.vector.memset(one[:], 1.0)
+        nc.scalar.activation(out=junk[:], in_=one[:], func=ACT.Sqrt)
+        nc.vector.memset(w_plane[:].bitcast(I32), 0)
+        for v in range(ROWS // PLANE):
+            nc.vector.memset(x_plane[v][:].bitcast(I32), 0)
+        nc.gpsimd.memset(ones[:], 1.0)
+
+        def scale_loads(plane, scales, n0, n1):
+            for r in range(4):
+                nc.sync.dma_start(
+                    out=plane[r:P:32, :, :].bitcast(I32),
+                    in_=scales[:, r:16:4, n0:n1].rearrange("g q n -> q g n").bitcast(I32),
+                )
+
+        def plane_loads(v):
+            for g in range(0, PASSES, 2):
+                for r in range(4):
+                    nc.sync.dma_start(
+                        out=x_plane[v][r:P:32, g : g + 2, :].bitcast(I32),
+                        in_=x_scales[g : g + 2, r:16:4, PLANE * v : PLANE * (v + 1)]
+                        .rearrange("g q n -> q g n")
+                        .bitcast(I32),
+                    )
+
+        def group_loads(u):
+            chunks, loads = GROUPS[u]
+            n0 = CH * chunks[0]
+            n1 = CH * (chunks[-1] + 1)
+            for g0, g1 in loads:
+                nc.sync.dma_start(
+                    out=x_codes[u][:, g0:g1, :].bitcast(I32),
+                    in_=x_words[g0:g1, :, 2 * n0 : 2 * n1].rearrange("g p n -> p g n").bitcast(I32),
+                )
+
+        for k in range(4):
+            nc.sync.dma_start(out=kv_sb[:, 2 * k : 2 * k + 2, :], in_=kv_v[:, 2 * k : 2 * k + 2, :])
+        nc.sync.dma_start(
+            out=w_codes[:].bitcast(I32),
+            in_=Wq_words.rearrange("g p n -> p g n").bitcast(I32),
+        )
+        scale_loads(w_plane, Wq_scales, 0, P)
+        plane_loads(0)
+        group_loads(0)
+        group_loads(1)
+        plane_loads(1)
+        group_loads(2)
+        group_loads(3)
+        group_loads(4)
+
+        d_ps = psum.tile([P, P], BF16, name="d_ps", tag="s", bufs=1)
+        nc.tensor.transpose(out=d_ps[:], in_=d_sb[:], identity=ident_bf[:])
+        nc.scalar.copy(out=dT_sb[:], in_=d_ps[:])
+
+        def kv_transposes(c):
+            k_ps = psum.tile([P, T, P], BF16, name="k_ps", tag="acc", bufs=5)
+            for t in range(T):
+                nc.tensor.transpose(
+                    out=k_ps[:, t, :], in_=kv_sb[:, c, P * t : P * (t + 1)], identity=ident_bf[:]
+                )
+            if c % 2 == 0:
+                nc.vector.tensor_copy(out=kvT_sb[c][:], in_=k_ps[:].rearrange("i t p -> i (t p)"))
+            else:
+                nc.scalar.copy(out=kvT_sb[c][:], in_=k_ps[:].rearrange("i t p -> i (t p)"))
+
+        def g_matmul(c):
+            g_ps = psum.tile([P, CH], F32, name="g_ps", tag="acc", bufs=5)
+            nc.tensor.matmul(out=g_ps[:], lhsT=dT_sb[:], rhs=kvT_sb[c][:], start=True, stop=True)
+            if c % 2 == 0:
+                nc.scalar.copy(out=gT_sb[c][:], in_=g_ps[:])
+            else:
+                nc.vector.tensor_copy(out=gT_sb[c][:], in_=g_ps[:])
+
+        kv_transposes(0)
+        kv_transposes(1)
+        for c in range(2, NCH):
+            kv_transposes(c)
+            g_matmul(c - 2)
+        g_matmul(NCH - 2)
+        g_matmul(NCH - 1)
+
+        nc.vector.tensor_scalar(out=eps_t[:], in0=one[:], scalar1=EPS, scalar2=None, op0=ALU.mult)
+        for k in range(2):
+            nc.vector.tensor_scalar(
+                out=sel[:, :, k], in0=blk[:, 0:P:Q], scalar1=1.0 / (P * P), scalar2=None, op0=ALU.mult
+            )
+
+        q_ps = {}
+        t_ps = {}
+        yT = {}
+        stat = {}
+
+        def mx_pass(u, c, g):
+            if g == 0:
+                q_new = psum.tile([P, CH], F32, name="q_ps", tag="acc", bufs=5)
+                q_ps[c] = q_new
+            o = CH * (c - GROUPS[u][0][0])
+            v = CH * c // PLANE
+            ov = CH * c - PLANE * v
+            nc.tensor.matmul_mx(
+                out=q_ps[c][:],
+                lhsT=w_codes[:, g, :].bitcast(FP4X4),
+                lhsT_scale=w_plane[:, g, :],
+                rhs=x_codes[u][:, g, 2 * o : 2 * (o + CH)].bitcast(FP4X4),
+                rhs_scale=x_plane[v][:, g, ov : ov + CH],
+                start=(g == 0),
+                stop=(g == PASSES - 1),
+            )
+
+        def product(u):
+            chunks = GROUPS[u][0]
+            st = work.tile([P, len(chunks) * T, 2], F32, name="stat", tag="stat", bufs=2)
+            stat[u] = st
+            for h, c in enumerate(chunks):
+                y_new = work.tile([P, CH], F32, name="yT", tag="yT", bufs=4)
+                yT[c] = y_new
+                y3 = y_new[:].rearrange("j (t p) -> j t p", t=T)
+                g3 = gT_sb[c][:].rearrange("j (t p) -> j t p", t=T)
+                for s in range(T):
+                    nc.vector.scalar_tensor_tensor(
+                        out=y3[:, :, Q * s : Q * (s + 1)],
+                        in0=q_ps[c][:, P * s : P * (s + 1)].rearrange("j (q t) -> j t q", t=T),
+                        scalar=bq_sb[:, 0:1],
+                        in1=g3[:, :, Q * s : Q * (s + 1)],
+                        op0=ALU.add,
+                        op1=ALU.mult,
+                        accum_out=st[:, h * T + s, 0:1],
+                    )
+                    sq = work.tile([P, T, Q], F32, name="sq", tag="sq", bufs=2)
+                    nc.scalar.activation(
+                        out=sq[:],
+                        in_=y3[:, :, Q * s : Q * (s + 1)],
+                        func=ACT.Square,
+                        accum_out=st[:, h * T + s, 1:2],
+                    )
+
+        def turn(u):
+            for c in GROUPS[u][0]:
+                t_new = psum.tile([P, T, P], F32, name="t_ps", tag="T", bufs=2)
+                t_ps[c] = t_new
+                for t in range(T):
+                    nc.tensor.transpose(
+                        out=t_new[:, t, :], in_=yT[c][:, P * t : P * (t + 1)], identity=ident_f[:]
+                    )
+
+        def normalise_and_store(u):
+            chunks = GROUPS[u][0]
+            n = len(chunks)
+            s_ps = psum.tile([P, n, T, 2], F32, name="s_ps", tag="s", bufs=1)
+            nc.tensor.matmul(
+                out=s_ps[:].rearrange("p n s k -> p (n s k)"),
+                lhsT=ones[:],
+                rhs=stat[u][:].rearrange("p s k -> p (s k)"),
+                start=True,
+                stop=True,
+            )
+            picked = work.tile([P, n, T, 2], F32, name="picked", tag="picked", bufs=2)
+            ms = work.tile([P, n, 2], F32, name="ms", tag="ms", bufs=2)
+            nv = work.tile([P, n], F32, name="nv", tag="nv", bufs=2)
+            sd = work.tile([P, n], F32, name="sd", tag="sd", bufs=2)
+            rstd = work.tile([P, n], F32, name="rstd", tag="rstd", bufs=2)
+            nb = work.tile([P, n], F32, name="nb", tag="nb", bufs=2)
+            for h in range(n):
+                nc.vector.tensor_tensor(out=picked[:, h, :, :], in0=s_ps[:, h, :, :], in1=sel[:], op=ALU.mult)
+            for h in range(n):
+                nc.vector.tensor_reduce(
+                    out=ms[:, h, :], in_=picked[:, h, :, :].rearrange("p s k -> p k s"), axis=AX.X, op=ALU.add
+                )
+            for h in range(n):
+                nc.vector.scalar_tensor_tensor(
+                    out=nv[:, h : h + 1],
+                    in0=ms[:, h, 0:1],
+                    scalar=ms[:, h, 0:1],
+                    in1=ms[:, h, 1:2],
+                    op0=ALU.mult,
+                    op1=ALU.subtract,
+                )
+            nc.scalar.activation(out=sd[:], in_=nv[:], func=ACT.Sqrt, bias=eps_t[:, 0:1], scale=-1.0)
+            nc.vector.reciprocal(out=rstd[:], in_=sd[:])
+            nc.vector.scalar_tensor_tensor(
+                out=nb[:], in0=ms[:, :, 0], scalar=-1.0, in1=rstd[:], op0=ALU.mult, op1=ALU.mult
+            )
+            for h, c in enumerate(chunks):
+                nc.scalar.activation(
+                    out=o_sb[c][:],
+                    in_=t_ps[c][:].rearrange("p t j -> p (t j)"),
+                    func=ACT.Identity,
+                    bias=nb[:, h : h + 1],
+                    scale=rstd[:, h : h + 1],
+                )
+                nc.sync.dma_start(out=out_v[:, c, :], in_=o_sb[c][:])
+
+        todo = {}
+        count = 0
+        for u, (chunks, loads) in enumerate(GROUPS):
+            count += PASSES * len(chunks)
+            todo.setdefault(count, []).append((product, u))
+            todo.setdefault(count + TURN_AFTER, []).append((turn, u))
+            todo.setdefault(count + NORM_AFTER, []).append((normalise_and_store, u))
+        done = 0
+        for u, (chunks, loads) in enumerate(GROUPS):
+            for g in range(PASSES):
+                for c in chunks:
+                    mx_pass(u, c, g)
+                    done += 1
+                    for stage, w in todo.get(done, []):
+                        stage(w)
+        for k in sorted(todo):
+            if k > done:
+                for stage, w in todo[k]:
+                    stage(w)

@@ -19,7 +19,7 @@ CH = 512
 NCH = ROWS // CH
 T = CH // P
 Q = P // T
-PLANE = 2048
+HP = 4
 EPS = 1e-5
 TURN_AFTER = 8
 NORM_AFTER = 10
@@ -70,8 +70,8 @@ def tile_parallelretention_pb_kernel(
             xc = const.tile([P, PASSES, 2 * cols], U8, name="x_codes%d" % u, align_bytes=64)
             x_codes.append(xc)
         x_plane = []
-        for v in range(ROWS // PLANE):
-            xp = const.tile([P, PASSES, PLANE], U8, name="x_plane%d" % v, align_bytes=64)
+        for v in range(PASSES // HP):
+            xp = const.tile([P, HP, ROWS], U8, name="x_plane%d" % v, align_bytes=64)
             x_plane.append(xp)
         kvT_sb = []
         gT_sb = []
@@ -92,7 +92,7 @@ def tile_parallelretention_pb_kernel(
         nc.vector.memset(one[:], 1.0)
         nc.scalar.activation(out=junk[:], in_=one[:], func=ACT.Sqrt)
         nc.vector.memset(w_plane[:].bitcast(I32), 0)
-        for v in range(ROWS // PLANE):
+        for v in range(PASSES // HP):
             nc.vector.memset(x_plane[v][:].bitcast(I32), 0)
         nc.gpsimd.memset(ones[:], 1.0)
 
@@ -104,14 +104,11 @@ def tile_parallelretention_pb_kernel(
                 )
 
         def plane_loads(v):
-            for g in range(0, PASSES, 2):
-                for r in range(4):
-                    nc.sync.dma_start(
-                        out=x_plane[v][r:P:32, g : g + 2, :].bitcast(I32),
-                        in_=x_scales[g : g + 2, r:16:4, PLANE * v : PLANE * (v + 1)]
-                        .rearrange("g q n -> q g n")
-                        .bitcast(I32),
-                    )
+            for r in range(4):
+                nc.sync.dma_start(
+                    out=x_plane[v][r:P:32, :, :].bitcast(I32),
+                    in_=x_scales[HP * v : HP * (v + 1), r:16:4, :].rearrange("g q n -> q g n").bitcast(I32),
+                )
 
         def group_loads(u):
             chunks, loads = GROUPS[u]
@@ -131,9 +128,9 @@ def tile_parallelretention_pb_kernel(
         )
         scale_loads(w_plane, Wq_scales, 0, P)
         plane_loads(0)
+        plane_loads(1)
         group_loads(0)
         group_loads(1)
-        plane_loads(1)
         group_loads(2)
         group_loads(3)
         group_loads(4)
@@ -185,14 +182,12 @@ def tile_parallelretention_pb_kernel(
                 q_new = psum.tile([P, CH], F32, name="q_ps", tag="acc", bufs=5)
                 q_ps[c] = q_new
             o = CH * (c - GROUPS[u][0][0])
-            v = CH * c // PLANE
-            ov = CH * c - PLANE * v
             nc.tensor.matmul_mx(
                 out=q_ps[c][:],
                 lhsT=w_codes[:, g, :].bitcast(FP4X4),
                 lhsT_scale=w_plane[:, g, :],
                 rhs=x_codes[u][:, g, 2 * o : 2 * (o + CH)].bitcast(FP4X4),
-                rhs_scale=x_plane[v][:, g, ov : ov + CH],
+                rhs_scale=x_plane[g // HP][:, g % HP, CH * c : CH * (c + 1)],
                 start=(g == 0),
                 stop=(g == PASSES - 1),
             )

@@ -104,11 +104,12 @@ def tile_parallelretention_pb_kernel(
                 )
 
         def plane_loads(v):
-            for r in range(4):
-                nc.sync.dma_start(
-                    out=x_plane[v][r:P:32, :, :].bitcast(I32),
-                    in_=x_scales[HP * v : HP * (v + 1), r:16:4, :].rearrange("g q n -> q g n").bitcast(I32),
-                )
+            for g in range(HP):
+                for r in range(4):
+                    nc.sync.dma_start(
+                        out=x_plane[v][r:P:32, g, :].bitcast(I32),
+                        in_=x_scales[HP * v + g, r:16:4, :].bitcast(I32),
+                    )
 
         def group_loads(u):
             chunks, loads = GROUPS[u]

@@ -23,10 +23,11 @@ HP = 4
 EPS = 1e-5
 TURN_AFTER = 8
 NORM_AFTER = 10
+ON_VECTOR = (1, 3, 5, 7)
 FLOPS = 2 * 4096 * 4096 * 128 + 2 * 4096 * 128 * 128
 
 GROUPS = (
-    ((0, 1), ((0, 2), (2, 4), (4, 6), (6, 8))),
+    ((0, 1), ((0, 1), (1, 2), (2, 4), (4, 6), (6, 8))),
     ((2, 3), ((0, 2), (2, 4), (4, 6), (6, 8))),
     ((4, 5), ((0, 2), (2, 4), (4, 6), (6, 8))),
     ((6,), ((0, 2), (2, 4), (4, 6), (6, 8))),
@@ -57,7 +58,7 @@ def tile_parallelretention_pb_kernel(
         junk = const.tile([P, 1], F32, name="junk")
         eps_t = const.tile([P, 1], F32, name="eps_t")
         ones = const.tile([P, P], F32, name="ones")
-        sel = const.tile([P, T, 2], F32, name="sel")
+        sel = const.tile([P, T], F32, name="sel")
         d_sb = const.tile([P, P], BF16, name="d_sb")
         dT_sb = const.tile([P, P], BF16, name="dT_sb")
         bq_sb = const.tile([P, 1], BF16, name="bq_sb")
@@ -90,10 +91,10 @@ def tile_parallelretention_pb_kernel(
         with nc.allow_non_contiguous_dma(reason="one bias value to a partition"):
             nc.scalar.dma_start(out=bq_sb[:], in_=bq.rearrange("(p o) -> p o", o=1))
         nc.vector.memset(one[:], 1.0)
-        nc.scalar.activation(out=junk[:], in_=one[:], func=ACT.Sqrt)
+        nc.scalar.activation(out=junk[:], in_=one[:], func=ACT.Abs_reciprocal_sqrt)
         nc.vector.memset(w_plane[:].bitcast(I32), 0)
-        for v in range(PASSES // HP):
-            nc.vector.memset(x_plane[v][:].bitcast(I32), 0)
+        nc.vector.memset(x_plane[0][:].bitcast(I32), 0)
+        nc.vector.memset(x_plane[1][:].bitcast(I32), 0)
         nc.gpsimd.memset(ones[:], 1.0)
 
         def scale_loads(plane, scales, n0, n1):
@@ -168,10 +169,7 @@ def tile_parallelretention_pb_kernel(
         g_matmul(NCH - 1)
 
         nc.vector.tensor_scalar(out=eps_t[:], in0=one[:], scalar1=EPS, scalar2=None, op0=ALU.mult)
-        for k in range(2):
-            nc.vector.tensor_scalar(
-                out=sel[:, :, k], in0=blk[:, 0:P:Q], scalar1=1.0 / (P * P), scalar2=None, op0=ALU.mult
-            )
+        nc.vector.tensor_scalar(out=sel[:], in0=blk[:, 0:P:Q], scalar1=1.0 / (P * P), scalar2=None, op0=ALU.mult)
 
         q_ps = {}
         t_ps = {}
@@ -240,18 +238,22 @@ def tile_parallelretention_pb_kernel(
                 start=True,
                 stop=True,
             )
-            picked = work.tile([P, n, T, 2], F32, name="picked", tag="picked", bufs=2)
+            scr = work.tile([P, n, 2, T], F32, name="scr", tag="scr", bufs=2)
             ms = work.tile([P, n, 2], F32, name="ms", tag="ms", bufs=2)
             nv = work.tile([P, n], F32, name="nv", tag="nv", bufs=2)
-            sd = work.tile([P, n], F32, name="sd", tag="sd", bufs=2)
             rstd = work.tile([P, n], F32, name="rstd", tag="rstd", bufs=2)
             nb = work.tile([P, n], F32, name="nb", tag="nb", bufs=2)
             for h in range(n):
-                nc.vector.tensor_tensor(out=picked[:, h, :, :], in0=s_ps[:, h, :, :], in1=sel[:], op=ALU.mult)
-            for h in range(n):
-                nc.vector.tensor_reduce(
-                    out=ms[:, h, :], in_=picked[:, h, :, :].rearrange("p s k -> p k s"), axis=AX.X, op=ALU.add
-                )
+                for k in range(2):
+                    nc.vector.scalar_tensor_tensor(
+                        out=scr[:, h, k, :],
+                        in0=s_ps[:, h, :, k],
+                        scalar=1.0,
+                        in1=sel[:],
+                        op0=ALU.mult,
+                        op1=ALU.mult,
+                        accum_out=ms[:, h, k : k + 1],
+                    )
             for h in range(n):
                 nc.vector.scalar_tensor_tensor(
                     out=nv[:, h : h + 1],
@@ -261,20 +263,42 @@ def tile_parallelretention_pb_kernel(
                     op0=ALU.mult,
                     op1=ALU.subtract,
                 )
-            nc.scalar.activation(out=sd[:], in_=nv[:], func=ACT.Sqrt, bias=eps_t[:, 0:1], scale=-1.0)
-            nc.vector.reciprocal(out=rstd[:], in_=sd[:])
-            nc.vector.scalar_tensor_tensor(
-                out=nb[:], in0=ms[:, :, 0], scalar=-1.0, in1=rstd[:], op0=ALU.mult, op1=ALU.mult
-            )
+            nc.scalar.activation(out=rstd[:], in_=nv[:], func=ACT.Abs_reciprocal_sqrt, bias=eps_t[:, 0:1], scale=-1.0)
             for h, c in enumerate(chunks):
-                nc.scalar.activation(
-                    out=o_sb[c][:],
-                    in_=t_ps[c][:].rearrange("p t j -> p (t j)"),
-                    func=ACT.Identity,
-                    bias=nb[:, h : h + 1],
-                    scale=rstd[:, h : h + 1],
-                )
-                nc.sync.dma_start(out=out_v[:, c, :], in_=o_sb[c][:])
+                if c in ON_VECTOR:
+                    pieces = 2 if c == NCH - 1 else 1
+                    w = CH // pieces
+                    for e in range(pieces):
+                        nc.vector.tensor_scalar(
+                            out=o_sb[c][:, w * e : w * (e + 1)],
+                            in0=t_ps[c][:].rearrange("p t j -> p (t j)")[:, w * e : w * (e + 1)],
+                            scalar1=ms[:, h, 0:1],
+                            scalar2=rstd[:, h : h + 1],
+                            op0=ALU.subtract,
+                            op1=ALU.mult,
+                        )
+                        if pieces > 1:
+                            nc.sync.dma_start(out=out_v[:, c, w * e : w * (e + 1)], in_=o_sb[c][:, w * e : w * (e + 1)])
+            for h, c in enumerate(chunks):
+                if c not in ON_VECTOR:
+                    nc.vector.scalar_tensor_tensor(
+                        out=nb[:, h : h + 1],
+                        in0=ms[:, h, 0:1],
+                        scalar=-1.0,
+                        in1=rstd[:, h : h + 1],
+                        op0=ALU.mult,
+                        op1=ALU.mult,
+                    )
+                    nc.scalar.activation(
+                        out=o_sb[c][:],
+                        in_=t_ps[c][:].rearrange("p t j -> p (t j)"),
+                        func=ACT.Identity,
+                        bias=nb[:, h : h + 1],
+                        scale=rstd[:, h : h + 1],
+                    )
+            for c in chunks:
+                if c != NCH - 1:
+                    nc.sync.dma_start(out=out_v[:, c, :], in_=o_sb[c][:])
 
         todo = {}
         count = 0

@@ -62,6 +62,7 @@ def tile_parallelretention_pb_kernel(
         d_sb = const.tile([P, P], BF16, name="d_sb")
         dT_sb = const.tile([P, P], BF16, name="dT_sb")
         bq_sb = const.tile([P, 1], BF16, name="bq_sb")
+        bq_row = const.tile([P, P], BF16, name="bq_row")
         kv_sb = const.tile([P, NCH, CH], BF16, name="kv_sb")
         w_codes = const.tile([P, PASSES, 2 * P], U8, name="w_codes", align_bytes=64)
         w_plane = const.tile([P, PASSES, P], U8, name="w_plane", align_bytes=64)
@@ -88,8 +89,8 @@ def tile_parallelretention_pb_kernel(
         ctx.enter_context(tc.manual_schedule())
 
         nc.scalar.dma_start(out=d_sb[:], in_=decay_mask[0])
-        with nc.allow_non_contiguous_dma(reason="one bias value to a partition"):
-            nc.scalar.dma_start(out=bq_sb[:], in_=bq.rearrange("(p o) -> p o", o=1))
+        nc.gpsimd.memset(bq_row[:], 0.0)
+        nc.scalar.dma_start(out=bq_row[0:1, :], in_=bq.rearrange("(o j) -> o j", o=1))
         nc.vector.memset(one[:], 1.0)
         nc.scalar.activation(out=junk[:], in_=one[:], func=ACT.Abs_reciprocal_sqrt)
         nc.vector.memset(w_plane[:].bitcast(I32), 0)
@@ -140,6 +141,9 @@ def tile_parallelretention_pb_kernel(
         d_ps = psum.tile([P, P], BF16, name="d_ps", tag="s", bufs=1)
         nc.tensor.transpose(out=d_ps[:], in_=d_sb[:], identity=ident_bf[:])
         nc.scalar.copy(out=dT_sb[:], in_=d_ps[:])
+        b_ps = psum.tile([P, P], BF16, name="b_ps", tag="s", bufs=1)
+        nc.tensor.transpose(out=b_ps[:], in_=bq_row[:], identity=ident_bf[:])
+        nc.scalar.copy(out=bq_sb[:], in_=b_ps[:, 0:1])
 
         def kv_transposes(c):
             k_ps = psum.tile([P, T, P], BF16, name="k_ps", tag="acc", bufs=5)

@@ -19,7 +19,7 @@ CH = 512
 NCH = ROWS // CH
 T = CH // P
 Q = P // T
-HP = 4
+HP = 8
 EPS = 1e-5
 TURN_AFTER = 8
 NORM_AFTER = 10
@@ -73,7 +73,7 @@ def tile_parallelretention_pb_kernel(
             x_codes.append(xc)
         x_plane = []
         for v in range(PASSES // HP):
-            xp = const.tile([P, HP, ROWS], U8, name="x_plane%d" % v, align_bytes=64)
+            xp = const.tile([P, HP, ROWS], U8, name="x_plane%d" % v, align_bytes=256)
             x_plane.append(xp)
         kvT_sb = []
         gT_sb = []
@@ -95,7 +95,6 @@ def tile_parallelretention_pb_kernel(
         nc.scalar.activation(out=junk[:], in_=one[:], func=ACT.Abs_reciprocal_sqrt)
         nc.vector.memset(w_plane[:].bitcast(I32), 0)
         nc.vector.memset(x_plane[0][:].bitcast(I32), 0)
-        nc.vector.memset(x_plane[1][:].bitcast(I32), 0)
         nc.gpsimd.memset(ones[:], 1.0)
 
         def scale_loads(plane, scales, n0, n1):
@@ -106,11 +105,13 @@ def tile_parallelretention_pb_kernel(
                 )
 
         def plane_loads(v):
-            for g in range(HP):
-                for r in range(4):
+            for r in range(4):
+                for quad in (0, 2, 1, 3):
+                    p = 32 * quad + r
+                    q = 4 * quad + r
                     nc.sync.dma_start(
-                        out=x_plane[v][r:P:32, g, :].bitcast(I32),
-                        in_=x_scales[HP * v + g, r:16:4, :].bitcast(I32),
+                        out=x_plane[v][p : p + 1, :, :].bitcast(I32),
+                        in_=x_scales[:, q : q + 1, :].rearrange("g q n -> q g n").bitcast(I32),
                     )
 
         def group_loads(u):
@@ -131,7 +132,6 @@ def tile_parallelretention_pb_kernel(
         )
         scale_loads(w_plane, Wq_scales, 0, P)
         plane_loads(0)
-        plane_loads(1)
         group_loads(0)
         group_loads(1)
         group_loads(2)

@@ -104,15 +104,20 @@ def tile_parallelretention_pb_kernel(
                     in_=scales[:, r:16:4, n0:n1].rearrange("g q n -> q g n").bitcast(I32),
                 )
 
+        def row_load(v, quad, r, g0, g1):
+            p = 32 * quad + r
+            q = 4 * quad + r
+            nc.sync.dma_start(
+                out=x_plane[v][p : p + 1, g0:g1, :].bitcast(I32),
+                in_=x_scales[g0:g1, q : q + 1, :].rearrange("g q n -> q g n").bitcast(I32),
+            )
+
         def plane_loads(v):
-            for r in range(4):
-                for quad in (0, 2, 1, 3):
-                    p = 32 * quad + r
-                    q = 4 * quad + r
-                    nc.sync.dma_start(
-                        out=x_plane[v][p : p + 1, :, :].bitcast(I32),
-                        in_=x_scales[:, q : q + 1, :].rearrange("g q n -> q g n").bitcast(I32),
-                    )
+            rows = [(quad, r) for r in range(4) for quad in (0, 2, 1, 3)]
+            row_load(v, rows[0][0], rows[0][1], 0, PASSES // 2)
+            for quad, r in rows[1:]:
+                row_load(v, quad, r, 0, PASSES)
+            row_load(v, rows[0][0], rows[0][1], PASSES // 2, PASSES)
 
         def group_loads(u):
             chunks, loads = GROUPS[u]

from contextlib import ExitStack

import concourse.mybir as mybir
from concourse.masks import make_block_diagonal, make_identity

F32 = mybir.dt.float32
BF16 = mybir.dt.bfloat16
U8 = mybir.dt.uint8
I32 = mybir.dt.int32
FP4X4 = mybir.dt.float4_e2m1fn_x4
ALU = mybir.AluOpType
ACT = mybir.ActivationFunctionType
AX = mybir.AxisListType

P = 128
PASSES = 8
ROWS = 4096
CH = 512
NCH = ROWS // CH
T = CH // P
Q = P // T
HP = 8
EPS = 1e-5
TURN_AFTER = 8
NORM_AFTER = 10
ON_VECTOR = (1, 3, 5, 7)
FLOPS = 2 * 4096 * 4096 * 128 + 2 * 4096 * 128 * 128

GROUPS = (
    ((0, 1), ((0, 1), (1, 2), (2, 4), (4, 6), (6, 8))),
    ((2, 3), ((0, 2), (2, 4), (4, 6), (6, 8))),
    ((4, 5), ((0, 2), (2, 4), (4, 6), (6, 8))),
    ((6,), ((0, 2), (2, 4), (4, 6), (6, 8))),
    ((7,), ((0, 2), (2, 4), (4, 6), (6, 7), (7, 8))),
)


def tile_parallelretention_pb_kernel(
    tc, x_words, x_scales, Wq_words, Wq_scales, bq, kv, decay_mask, out
):
    nc = tc.nc
    kv_v = kv.rearrange("b h l i -> (b h l) i").rearrange("(c p t) i -> p c (t i)", p=P, t=T)
    out_v = out.rearrange("b l j -> (b l) j").rearrange("(c p t) j -> p c (t j)", p=P, t=T)

    with ExitStack() as ctx:
        const = ctx.enter_context(tc.tile_pool(name="const", bufs=1))
        work = ctx.enter_context(tc.tile_pool(name="work", bufs=3))
        psum = ctx.enter_context(tc.psum_pool(name="psum", bufs=1))

        ident_bf = const.tile([P, P], BF16, name="ident_bf")
        ident_f = const.tile([P, P], F32, name="ident_f")
        blk = const.tile([P, P], F32, name="blk")
        make_identity(nc, ident_bf[:])
        make_identity(nc, ident_f[:])
        make_block_diagonal(nc, blk[:], Q)

        one = const.tile([P, 1], F32, name="one")
        junk = const.tile([P, 1], F32, name="junk")
        eps_t = const.tile([P, 1], F32, name="eps_t")
        ones = const.tile([P, P], F32, name="ones")
        sel = const.tile([P, T], F32, name="sel")
        d_sb = const.tile([P, P], BF16, name="d_sb")
        dT_sb = const.tile([P, P], BF16, name="dT_sb")
        bq_sb = const.tile([P, 1], BF16, name="bq_sb")
        bq_row = const.tile([P, P], BF16, name="bq_row")
        kv_sb = const.tile([P, NCH, CH], BF16, name="kv_sb")
        w_codes = const.tile([P, PASSES, 2 * P], U8, name="w_codes", align_bytes=64)
        w_plane = const.tile([P, PASSES, P], U8, name="w_plane", align_bytes=64)
        x_codes = []
        for u, (chunks, loads) in enumerate(GROUPS):
            cols = CH * len(chunks)
            xc = const.tile([P, PASSES, 2 * cols], U8, name="x_codes%d" % u, align_bytes=64)
            x_codes.append(xc)
        x_plane = []
        for v in range(PASSES // HP):
            xp = const.tile([P, HP, ROWS], U8, name="x_plane%d" % v, align_bytes=256)
            x_plane.append(xp)
        kvT_sb = []
        gT_sb = []
        o_sb = []
        for c in range(NCH):
            kt = const.tile([P, CH], BF16, name="kvT_sb%d" % c)
            gt = const.tile([P, CH], F32, name="gT_sb%d" % c)
            ot = const.tile([P, CH], F32, name="o_sb%d" % c)
            kvT_sb.append(kt)
            gT_sb.append(gt)
            o_sb.append(ot)

        ctx.enter_context(tc.manual_schedule())

        nc.scalar.dma_start(out=d_sb[:], in_=decay_mask[0])
        nc.gpsimd.memset(bq_row[:], 0.0)
        nc.scalar.dma_start(out=bq_row[0:1, :], in_=bq.rearrange("(o j) -> o j", o=1))
        nc.vector.memset(one[:], 1.0)
        nc.scalar.activation(out=junk[:], in_=one[:], func=ACT.Abs_reciprocal_sqrt)
        nc.vector.memset(w_plane[:].bitcast(I32), 0)
        nc.vector.memset(x_plane[0][:].bitcast(I32), 0)
        nc.gpsimd.memset(ones[:], 1.0)

        def scale_loads(plane, scales, n0, n1):
            for r in range(4):
                nc.sync.dma_start(
                    out=plane[r:P:32, :, :].bitcast(I32),
                    in_=scales[:, r:16:4, n0:n1].rearrange("g q n -> q g n").bitcast(I32),
                )

        def row_load(v, quad, r, g0, g1):
            p = 32 * quad + r
            q = 4 * quad + r
            nc.sync.dma_start(
                out=x_plane[v][p : p + 1, g0:g1, :].bitcast(I32),
                in_=x_scales[g0:g1, q : q + 1, :].rearrange("g q n -> q g n").bitcast(I32),
            )

        def plane_loads(v):
            rows = [(quad, r) for r in range(4) for quad in (0, 2, 1, 3)]
            row_load(v, rows[0][0], rows[0][1], 0, PASSES // 2)
            for quad, r in rows[1:]:
                row_load(v, quad, r, 0, PASSES)
            row_load(v, rows[0][0], rows[0][1], PASSES // 2, PASSES)

        def group_loads(u):
            chunks, loads = GROUPS[u]
            n0 = CH * chunks[0]
            n1 = CH * (chunks[-1] + 1)
            for g0, g1 in loads:
                nc.sync.dma_start(
                    out=x_codes[u][:, g0:g1, :].bitcast(I32),
                    in_=x_words[g0:g1, :, 2 * n0 : 2 * n1].rearrange("g p n -> p g n").bitcast(I32),
                )

        for k in range(4):
            nc.sync.dma_start(out=kv_sb[:, 2 * k : 2 * k + 2, :], in_=kv_v[:, 2 * k : 2 * k + 2, :])
        nc.sync.dma_start(
            out=w_codes[:].bitcast(I32),
            in_=Wq_words.rearrange("g p n -> p g n").bitcast(I32),
        )
        scale_loads(w_plane, Wq_scales, 0, P)
        plane_loads(0)
        group_loads(0)
        group_loads(1)
        group_loads(2)
        group_loads(3)
        group_loads(4)

        d_ps = psum.tile([P, P], BF16, name="d_ps", tag="s", bufs=1)
        nc.tensor.transpose(out=d_ps[:], in_=d_sb[:], identity=ident_bf[:])
        nc.scalar.copy(out=dT_sb[:], in_=d_ps[:])
        b_ps = psum.tile([P, P], BF16, name="b_ps", tag="s", bufs=1)
        nc.tensor.transpose(out=b_ps[:], in_=bq_row[:], identity=ident_bf[:])
        nc.scalar.copy(out=bq_sb[:], in_=b_ps[:, 0:1])

        def kv_transposes(c):
            k_ps = psum.tile([P, T, P], BF16, name="k_ps", tag="acc", bufs=5)
            for t in range(T):
                nc.tensor.transpose(
                    out=k_ps[:, t, :], in_=kv_sb[:, c, P * t : P * (t + 1)], identity=ident_bf[:]
                )
            if c % 2 == 0:
                nc.vector.tensor_copy(out=kvT_sb[c][:], in_=k_ps[:].rearrange("i t p -> i (t p)"))
            else:
                nc.scalar.copy(out=kvT_sb[c][:], in_=k_ps[:].rearrange("i t p -> i (t p)"))

        def g_matmul(c):
            g_ps = psum.tile([P, CH], F32, name="g_ps", tag="acc", bufs=5)
            nc.tensor.matmul(out=g_ps[:], lhsT=dT_sb[:], rhs=kvT_sb[c][:], start=True, stop=True)
            if c % 2 == 0:
                nc.scalar.copy(out=gT_sb[c][:], in_=g_ps[:])
            else:
                nc.vector.tensor_copy(out=gT_sb[c][:], in_=g_ps[:])

        kv_transposes(0)
        kv_transposes(1)
        for c in range(2, NCH):
            kv_transposes(c)
            g_matmul(c - 2)
        g_matmul(NCH - 2)
        g_matmul(NCH - 1)

        nc.vector.tensor_scalar(out=eps_t[:], in0=one[:], scalar1=EPS, scalar2=None, op0=ALU.mult)
        nc.vector.tensor_scalar(out=sel[:], in0=blk[:, 0:P:Q], scalar1=1.0 / (P * P), scalar2=None, op0=ALU.mult)

        q_ps = {}
        t_ps = {}
        yT = {}
        stat = {}

        def mx_pass(u, c, g):
            if g == 0:
                q_new = psum.tile([P, CH], F32, name="q_ps", tag="acc", bufs=5)
                q_ps[c] = q_new
            o = CH * (c - GROUPS[u][0][0])
            nc.tensor.matmul_mx(
                out=q_ps[c][:],
                lhsT=w_codes[:, g, :].bitcast(FP4X4),
                lhsT_scale=w_plane[:, g, :],
                rhs=x_codes[u][:, g, 2 * o : 2 * (o + CH)].bitcast(FP4X4),
                rhs_scale=x_plane[g // HP][:, g % HP, CH * c : CH * (c + 1)],
                start=(g == 0),
                stop=(g == PASSES - 1),
            )

        def product(u):
            chunks = GROUPS[u][0]
            st = work.tile([P, len(chunks) * T, 2], F32, name="stat", tag="stat", bufs=2)
            stat[u] = st
            for h, c in enumerate(chunks):
                y_new = work.tile([P, CH], F32, name="yT", tag="yT", bufs=4)
                yT[c] = y_new
                y3 = y_new[:].rearrange("j (t p) -> j t p", t=T)
                g3 = gT_sb[c][:].rearrange("j (t p) -> j t p", t=T)
                for s in range(T):
                    nc.vector.scalar_tensor_tensor(
                        out=y3[:, :, Q * s : Q * (s + 1)],
                        in0=q_ps[c][:, P * s : P * (s + 1)].rearrange("j (q t) -> j t q", t=T),
                        scalar=bq_sb[:, 0:1],
                        in1=g3[:, :, Q * s : Q * (s + 1)],
                        op0=ALU.add,
                        op1=ALU.mult,
                        accum_out=st[:, h * T + s, 0:1],
                    )
                    sq = work.tile([P, T, Q], F32, name="sq", tag="sq", bufs=2)
                    nc.scalar.activation(
                        out=sq[:],
                        in_=y3[:, :, Q * s : Q * (s + 1)],
                        func=ACT.Square,
                        accum_out=st[:, h * T + s, 1:2],
                    )

        def turn(u):
            for c in GROUPS[u][0]:
                t_new = psum.tile([P, T, P], F32, name="t_ps", tag="T", bufs=2)
                t_ps[c] = t_new
                for t in range(T):
                    nc.tensor.transpose(
                        out=t_new[:, t, :], in_=yT[c][:, P * t : P * (t + 1)], identity=ident_f[:]
                    )

        def normalise_and_store(u):
            chunks = GROUPS[u][0]
            n = len(chunks)
            s_ps = psum.tile([P, n, T, 2], F32, name="s_ps", tag="s", bufs=1)
            nc.tensor.matmul(
                out=s_ps[:].rearrange("p n s k -> p (n s k)"),
                lhsT=ones[:],
                rhs=stat[u][:].rearrange("p s k -> p (s k)"),
                start=True,
                stop=True,
            )
            scr = work.tile([P, n, 2, T], F32, name="scr", tag="scr", bufs=2)
            ms = work.tile([P, n, 2], F32, name="ms", tag="ms", bufs=2)
            nv = work.tile([P, n], F32, name="nv", tag="nv", bufs=2)
            rstd = work.tile([P, n], F32, name="rstd", tag="rstd", bufs=2)
            nb = work.tile([P, n], F32, name="nb", tag="nb", bufs=2)
            for h in range(n):
                for k in range(2):
                    nc.vector.scalar_tensor_tensor(
                        out=scr[:, h, k, :],
                        in0=s_ps[:, h, :, k],
                        scalar=1.0,
                        in1=sel[:],
                        op0=ALU.mult,
                        op1=ALU.mult,
                        accum_out=ms[:, h, k : k + 1],
                    )
            for h in range(n):
                nc.vector.scalar_tensor_tensor(
                    out=nv[:, h : h + 1],
                    in0=ms[:, h, 0:1],
                    scalar=ms[:, h, 0:1],
                    in1=ms[:, h, 1:2],
                    op0=ALU.mult,
                    op1=ALU.subtract,
                )
            nc.scalar.activation(out=rstd[:], in_=nv[:], func=ACT.Abs_reciprocal_sqrt, bias=eps_t[:, 0:1], scale=-1.0)
            for h, c in enumerate(chunks):
                if c in ON_VECTOR:
                    pieces = 2 if c == NCH - 1 else 1
                    w = CH // pieces
                    for e in range(pieces):
                        nc.vector.tensor_scalar(
                            out=o_sb[c][:, w * e : w * (e + 1)],
                            in0=t_ps[c][:].rearrange("p t j -> p (t j)")[:, w * e : w * (e + 1)],
                            scalar1=ms[:, h, 0:1],
                            scalar2=rstd[:, h : h + 1],
                            op0=ALU.subtract,
                            op1=ALU.mult,
                        )
                        if pieces > 1:
                            nc.sync.dma_start(out=out_v[:, c, w * e : w * (e + 1)], in_=o_sb[c][:, w * e : w * (e + 1)])
            for h, c in enumerate(chunks):
                if c not in ON_VECTOR:
                    nc.vector.scalar_tensor_tensor(
                        out=nb[:, h : h + 1],
                        in0=ms[:, h, 0:1],
                        scalar=-1.0,
                        in1=rstd[:, h : h + 1],
                        op0=ALU.mult,
                        op1=ALU.mult,
                    )
                    nc.scalar.activation(
                        out=o_sb[c][:],
                        in_=t_ps[c][:].rearrange("p t j -> p (t j)"),
                        func=ACT.Identity,
                        bias=nb[:, h : h + 1],
                        scale=rstd[:, h : h + 1],
                    )
            for c in chunks:
                if c != NCH - 1:
                    nc.sync.dma_start(out=out_v[:, c, :], in_=o_sb[c][:])

        todo = {}
        count = 0
        for u, (chunks, loads) in enumerate(GROUPS):
            count += PASSES * len(chunks)
            todo.setdefault(count, []).append((product, u))
            todo.setdefault(count + TURN_AFTER, []).append((turn, u))
            todo.setdefault(count + NORM_AFTER, []).append((normalise_and_store, u))
        done = 0
        for u, (chunks, loads) in enumerate(GROUPS):
            for g in range(PASSES):
                for c in chunks:
                    mx_pass(u, c, g)
                    done += 1
                    for stage, w in todo.get(done, []):
                        stage(w)
        for k in sorted(todo):
            if k > done:
                for stage, w in todo[k]:
                    stage(w)
